import numpy as np
import ml_dtypes


def mxq(x, axis, fmt="e4m3"):
    dtype, down = {"e4m3": (ml_dtypes.float8_e4m3fn, 7), "e5m2": (ml_dtypes.float8_e5m2, 14)}[fmt]
    v = np.moveaxis(np.asarray(x, np.float32).astype(ml_dtypes.bfloat16).astype(np.float64), axis, -1)
    blocks = v.reshape(v.shape[:-1] + (-1, 32))
    amax = np.abs(blocks).max(-1, keepdims=True)
    byte = np.maximum(np.where(amax > 0, np.frexp(amax)[1] - 1 + 127, 0) - down, 1)
    scale = np.exp2(byte - 127.0)
    codes = (blocks / scale).astype(np.float32).astype(dtype).astype(np.float64)
    return np.moveaxis((codes * scale).reshape(v.shape), -1, axis)


WIDE = False


def mx_kscale(k):
    if not WIDE:
        return np.ones(k)
    levels = np.array([10, -10, 5, -5, 0])
    a = np.random.permutation(np.resize(levels, k // 512 * 4)).reshape(k // 512, 4)
    idx = np.arange(k)
    return np.exp2(a[idx // 512, idx % 128 // 32])


BF16 = ml_dtypes.bfloat16


def bf(x):
    return np.asarray(x, np.float32).astype(BF16)


def f64(x):
    return np.asarray(x).astype(np.float64)


B, C, H, W, S, HID, OC = 2, 128, 128, 128, 2, 1024, 128
H2, W2 = H // S, W // S
K1 = C * S * S
RESIDUAL = True


def setup_inputs():
    s = mx_kscale(K1)
    s = s / s.max()
    sx = np.broadcast_to(s.reshape(C, 1, S, 1, S), (C, H2, S, W2, S)).reshape(C, H, W)
    return {"x": bf(np.random.standard_normal((B, C, H, W)) * sx),
            "weight1": bf(np.random.standard_normal((HID, K1)) / np.sqrt(K1) / s),
            "bias1": bf(np.random.standard_normal(HID) * 0.2),
            "weight2": bf(np.random.standard_normal((OC, HID)) * 1.5 / np.sqrt(HID)),
            "bias2": bf(np.random.standard_normal(OC) * 0.2)}


def reference(x, weight1, bias1, weight2, bias2):
    x = f64(x)
    p = x.reshape(B, C, H2, S, W2, S)
    p = p.transpose(0, 2, 4, 1, 3, 5).reshape(B * H2 * W2, C * S * S)
    o1 = (mxq(p, 1, "e4m3") @ mxq(f64(weight1), 1, "e4m3").T) + f64(bias1)
    o2 = o1 * (1.0 / (1.0 + np.exp(-o1)))
    o3 = (mxq(o2, 1, "e4m3") @ mxq(f64(weight2), 1, "e4m3").T) + f64(bias2)
    out = o3.reshape(B, H2, W2, -1).transpose(0, 3, 1, 2)
    if RESIDUAL:
        pooled = x.reshape(B, C, H2, S, W2, S).mean(axis=(3, 5))
        n = out.shape[1] // C
        res = np.repeat(pooled, n, axis=1)
        out = out + res
    return out

@@ -1,0 +1,272 @@
+from contextlib import ExitStack
+
+import concourse.mybir as mybir
+from concourse.masks import make_identity
+
+F32 = mybir.dt.float32
+BF16 = mybir.dt.bfloat16
+U32 = mybir.dt.uint32
+U8 = mybir.dt.uint8
+FP8X4 = mybir.dt.float8_e4m3fn_x4
+ACT = mybir.ActivationFunctionType
+ALU = mybir.AluOpType
+
+P = 128
+TOK = 512
+NT = 16
+FLOPS = 2 * 8192 * 512 * 1024 + 2 * 8192 * 1024 * 128
+
+CHUNKS = ((1, 1, 2, 2, 2), (2, 2, 2, 2))
+
+
+def tile_memoryefficientpatchdownscale_t_kernel(tc, x, weight1, bias1, weight2, bias2, out):
+    nc = tc.nc
+    with ExitStack() as ctx:
+        consts = ctx.enter_context(tc.tile_pool(name="consts", bufs=1))
+        work = ctx.enter_context(tc.tile_pool(name="work", bufs=3))
+        psum = ctx.enter_context(tc.psum_pool(name="psum", bufs=1))
+        ctx.enter_context(tc.manual_schedule())
+
+        w1_src = weight1.rearrange("(g p j) k -> g p (j k)", g=2, p=P, j=4)
+        w1_raw = [consts.tile([P, 2048], BF16, name="w1_raw%d" % g) for g in range(2)]
+        x_loc = []
+        x_loads = []
+        for b in range(2):
+            first = 0
+            for count in CHUNKS[b]:
+                chunk = consts.tile([P, count * 2048], BF16, name="x_%d_%d" % (b, first))
+                src = x[b, :, 16 * first : 16 * (first + count), :].rearrange("c h w -> c (h w)")
+                x_loads.append((chunk, src))
+                for place in range(count):
+                    x_loc.append((chunk, place))
+                first += count
+        nc.sync.dma_start(out=w1_raw[0][:], in_=w1_src[0])
+        nc.sync.dma_start(out=x_loads[0][0][:], in_=x_loads[0][1])
+        nc.sync.dma_start(out=w1_raw[1][:], in_=w1_src[1])
+        for chunk, src in x_loads[1:]:
+            nc.sync.dma_start(out=chunk[:], in_=src)
+
+        b1_raw = consts.tile([P, 8], BF16, name="b1_raw")
+        nc.scalar.dma_start(
+            out=b1_raw[:].rearrange("p (g j) -> p g j", g=2),
+            in_=bias1.rearrange("(g p j) -> p g j", g=2, p=P, j=4),
+        )
+        w2_raw = consts.tile([P, 1024], BF16, name="w2_raw")
+        nc.scalar.dma_start(out=w2_raw[:], in_=weight2)
+        b2_raw = consts.tile([P, 1], BF16, name="b2_raw")
+        nc.scalar.dma_start(out=b2_raw[:], in_=bias2.rearrange("(p o) -> p o", o=1))
+
+        ident = consts.tile([P, P], F32, name="ident")
+        make_identity(nc, ident[:])
+        warm = consts.tile([P, 1], F32, name="warm")
+        nc.vector.memset(warm[:], 0.0)
+        warm_out = consts.tile([P, 1], F32, name="warm_out")
+        nc.scalar.activation(out=warm_out[:], in_=warm[:], func=ACT.Silu)
+        quarter = consts.tile([P, P], BF16, name="quarter")
+        nc.vector.tensor_scalar_mul(out=quarter[:], in0=ident[:], scalar1=0.25)
+
+        w1_grp = consts.tile([P, 4096], BF16, name="w1_grp", align_bytes=64)
+        w1_codes = consts.tile([P, 1024], U32, name="w1_codes", align_bytes=64)
+        w1_scales = consts.tile([P, 1024], U8, name="w1_scales", align_bytes=64)
+        w2_grp = consts.tile([P, 1024], BF16, name="w2_grp", align_bytes=64)
+        w2_codes = consts.tile([P, 256], U32, name="w2_codes", align_bytes=64)
+        w2_scales = consts.tile([P, 256], U8, name="w2_scales", align_bytes=64)
+        b1 = consts.tile([P, 8], F32, name="b1")
+        b2 = consts.tile([P, 1], F32, name="b2")
+
+        def bank(tag, bufs):
+            return psum.tile([P, TOK], F32, tag=tag, bufs=bufs, name=tag)
+
+        def flip(views, dst_words, copy):
+            pt = bank("o1", 5)
+            for s, view in enumerate(views):
+                nc.tensor.transpose(out=pt[:, s * P : (s + 1) * P], in_=view, identity=ident[:])
+            copy(
+                out=dst_words.rearrange("p (a h u) -> p a h u", a=2, u=2),
+                in_=pt[:].rearrange("p (a u h) -> p a h u", a=2, u=2),
+            )
+
+        def flip_w1(g, a, copy):
+            words = w1_raw[g][:].bitcast(F32).rearrange("p (j q u) -> p j u q", j=4, q=P, u=2)
+            views = [words[:, 2 * a + jl, u, :] for jl in range(2) for u in range(2)]
+            first = (4 * g + 2 * a) * 256
+            flip(views, w1_grp[:].bitcast(F32)[:, first : first + 512], copy)
+
+        def quant_w1(g):
+            nc.vector.quantize_mx(
+                out=w1_codes[:, g * 512 : (g + 1) * 512].bitcast(FP8X4),
+                scales=w1_scales[:, g * 512 : (g + 1) * 512],
+                in_=w1_grp[:, g * 2048 : (g + 1) * 2048],
+            )
+
+        x_codes = {}
+        x_grp = {}
+
+        def xr(n):
+            chunk, place = x_loc[n]
+            grp = work.tile([P, 2048], BF16, tag="x_grp", bufs=3, name="x_grp", align_bytes=64)
+            x_grp[n] = grp
+            nc.vector.tensor_copy(
+                out=grp[:].bitcast(F32).rearrange("p (i j u) -> p i j u", i=8, j=64, u=2),
+                in_=chunk[:]
+                .bitcast(F32)[:, place * 1024 : (place + 1) * 1024]
+                .rearrange("p (i u j) -> p i j u", i=8, u=2, j=64),
+            )
+
+        def xq(n):
+            codes = work.tile([P, TOK], U32, tag="x_codes", bufs=4, name="x_codes", align_bytes=64)
+            scales = work.tile([P, TOK], U8, tag="x_scales", bufs=4, name="x_scales", align_bytes=64)
+            x_codes[n] = (codes, scales)
+            nc.vector.quantize_mx(out=codes[:].bitcast(FP8X4), scales=scales[:], in_=x_grp[n][:])
+
+        o1 = {}
+        o2_raw = {}
+        o2_grp = {}
+        o2_codes = {}
+        pooled_ps = {}
+        pooled = {}
+        o3 = {}
+
+        def mm1(n, t):
+            acc = bank("o1", 5)
+            o1[(n, t)] = acc
+            codes, scales = x_codes[n]
+            nc.tensor.matmul_mx(
+                out=acc[:],
+                lhsT=w1_codes[:, t * P : (t + 1) * P].bitcast(FP8X4),
+                lhsT_scale=w1_scales[:, t * P : (t + 1) * P],
+                rhs=codes[:].bitcast(FP8X4),
+                rhs_scale=scales[:],
+                start=True,
+                stop=True,
+            )
+
+        def silu(n, t):
+            g, j = divmod(t, 4)
+            if j == 0:
+                o2_raw[(n, g)] = work.tile([P, 4, TOK], BF16, tag="o2_raw", bufs=4, name="o2_raw")
+            nc.scalar.activation(
+                out=o2_raw[(n, g)][:, j, :], in_=o1[(n, t)][:], func=ACT.Silu, bias=b1[:, t : t + 1], scale=1.0
+            )
+
+        def pool(n):
+            chunk, place = x_loc[n]
+            acc = bank("pp", 1)
+            pooled_ps[n] = acc
+            view = chunk[:, place * 2048 : (place + 1) * 2048].rearrange(
+                "p (i u j v) -> p u v i j", i=8, u=2, j=64, v=2
+            )
+            terms = 3 if n == NT - 1 else 4
+            for s in range(terms):
+                nc.tensor.matmul(
+                    out=acc[:].rearrange("p (i j) -> p i j", i=8),
+                    lhsT=quarter[:],
+                    rhs=view[:, s // 2, s % 2],
+                    start=(s == 0),
+                    stop=(s == terms - 1),
+                )
+
+        def pev(n):
+            res = work.tile([P, TOK], F32, tag="pooled", bufs=3, name="pooled")
+            pooled[n] = res
+            nc.scalar.activation(out=res[:], in_=pooled_ps[n][:], func=ACT.Identity, bias=b2[:, 0:1], scale=1.0)
+
+        def pev_last(n):
+            chunk, place = x_loc[n]
+            view = chunk[:, place * 2048 : (place + 1) * 2048].rearrange(
+                "p (i u j v) -> p u v i j", i=8, u=2, j=64, v=2
+            )
+            res = work.tile([P, TOK], F32, tag="pooled", bufs=3, name="pooled")
+            pooled[n] = res
+            nc.vector.scalar_tensor_tensor(
+                out=res[:].rearrange("p (i j) -> p i j", i=8),
+                in0=view[:, 1, 1],
+                scalar=0.25,
+                in1=pooled_ps[n][:].rearrange("p (i j) -> p i j", i=8),
+                op0=ALU.mult,
+                op1=ALU.add,
+            )
+
+        def oreg(n, g):
+            grp = work.tile([P, 2048], BF16, tag="o2_grp", bufs=3, name="o2_grp", align_bytes=64)
+            o2_grp[(n, g)] = grp
+            nc.vector.tensor_copy(
+                out=grp[:].rearrange("p (c i t) -> p c t i", i=4, t=4),
+                in_=o2_raw[(n, g)][:].rearrange("p t (c i) -> p c t i", i=4),
+            )
+
+        def oq(n, g):
+            codes = work.tile([P, TOK], U32, tag="o2_codes", bufs=4, name="o2_codes", align_bytes=64)
+            scales = work.tile([P, TOK], U8, tag="o2_scales", bufs=4, name="o2_scales", align_bytes=64)
+            o2_codes[(n, g)] = (codes, scales)
+            nc.vector.quantize_mx(out=codes[:].bitcast(FP8X4), scales=scales[:], in_=o2_grp[(n, g)][:])
+
+        def mm2(n):
+            acc = bank("o3", 2)
+            o3[n] = acc
+            for g in range(2):
+                codes, scales = o2_codes[(n, g)]
+                nc.tensor.matmul_mx(
+                    out=acc[:],
+                    lhsT=w2_codes[:, g * P : (g + 1) * P].bitcast(FP8X4),
+                    lhsT_scale=w2_scales[:, g * P : (g + 1) * P],
+                    rhs=codes[:].bitcast(FP8X4),
+                    rhs_scale=scales[:],
+                    start=(g == 0),
+                    stop=(g == 1),
+                )
+
+        def finish(n):
+            res = work.tile([P, TOK], F32, tag="res", bufs=4, name="res")
+            if n == NT - 1:
+                nc.vector.scalar_tensor_tensor(
+                    out=res[:], in0=o3[n][:], scalar=b2[:, 0:1], in1=pooled[n][:], op0=ALU.add, op1=ALU.add
+                )
+            else:
+                nc.vector.tensor_tensor(out=res[:], in0=o3[n][:], in1=pooled[n][:], op=ALU.add)
+            b, r = divmod(n, 8)
+            nc.sync.dma_start(out=out[b, :, 8 * r : 8 * r + 8, :].rearrange("c i j -> c (i j)"), in_=res[:])
+
+        flip_w1(0, 0, nc.scalar.copy)
+        flip_w1(0, 1, nc.scalar.copy)
+        xr(0)
+        xq(0)
+        quant_w1(0)
+        nc.vector.tensor_copy(out=b1[:], in_=b1_raw[:])
+        flip_w1(1, 0, nc.vector.tensor_copy)
+        flip_w1(1, 1, nc.vector.tensor_copy)
+        xr(1)
+        quant_w1(1)
+        xq(1)
+        w2_words = w2_raw[:].bitcast(F32).rearrange("p (g q u) -> p g u q", g=2, q=P, u=2)
+        flip([w2_words[:, g, u, :] for g in range(2) for u in range(2)], w2_grp[:].bitcast(F32), nc.vector.tensor_copy)
+        nc.vector.tensor_copy(out=b2[:], in_=b2_raw[:])
+        nc.vector.quantize_mx(out=w2_codes[:].bitcast(FP8X4), scales=w2_scales[:], in_=w2_grp[:])
+
+        for n in range(NT + 1):
+            if n < NT:
+                for t in range(4):
+                    mm1(n, t)
+                    silu(n, t)
+                oreg(n, 0)
+                if n + 2 < NT:
+                    xr(n + 2)
+                oq(n, 0)
+                if n + 2 < NT:
+                    xq(n + 2)
+                for t in range(4, 8):
+                    mm1(n, t)
+                    silu(n, t)
+                pool(n)
+                if n < NT - 1:
+                    pev(n)
+            if n >= 1:
+                mm2(n - 1)
+            if n < NT:
+                oreg(n, 1)
+            if n == NT:
+                pev_last(n - 1)
+            if n >= 1:
+                finish(n - 1)
+            if n < NT:
+                oq(n, 1)

@@ -14,9 +14,11 @@ ALU = mybir.AluOpType
 P = 128
 TOK = 512
 NT = 16
+AHEAD = 3
 FLOPS = 2 * 8192 * 512 * 1024 + 2 * 8192 * 1024 * 128
 
-CHUNKS = ((1, 1, 2, 2, 2), (2, 2, 2, 2))
+CHUNKS = ((1, 1, 1, 1, 2, 2), (2, 2, 2, 2))
+POOLED_BY_VECTOR = (14,)
 
 
 def tile_memoryefficientpatchdownscale_t_kernel(tc, x, weight1, bias1, weight2, bias2, out):
@@ -29,6 +31,9 @@ def tile_memoryefficientpatchdownscale_t_kernel(tc, x, weight1, bias1, weight2, 
 
         w1_src = weight1.rearrange("(g p j) k -> g p (j k)", g=2, p=P, j=4)
         w1_raw = [consts.tile([P, 2048], BF16, name="w1_raw%d" % g) for g in range(2)]
+        w2_raw = consts.tile([P, 1024], BF16, name="w2_raw")
+        b1_raw = consts.tile([P, 8], BF16, name="b1_raw")
+        b2_raw = consts.tile([P, 1], BF16, name="b2_raw")
         x_loc = []
         x_loads = []
         for b in range(2):
@@ -40,21 +45,27 @@ def tile_memoryefficientpatchdownscale_t_kernel(tc, x, weight1, bias1, weight2, 
                 for place in range(count):
                     x_loc.append((chunk, place))
                 first += count
-        nc.sync.dma_start(out=w1_raw[0][:], in_=w1_src[0])
-        nc.sync.dma_start(out=x_loads[0][0][:], in_=x_loads[0][1])
-        nc.sync.dma_start(out=w1_raw[1][:], in_=w1_src[1])
-        for chunk, src in x_loads[1:]:
-            nc.sync.dma_start(out=chunk[:], in_=src)
 
-        b1_raw = consts.tile([P, 8], BF16, name="b1_raw")
+        def load_w1(q):
+            g, a = divmod(q, 2)
+            nc.sync.dma_start(out=w1_raw[g][:, a * 1024 : (a + 1) * 1024], in_=w1_src[g][:, a * 1024 : (a + 1) * 1024])
+
         nc.scalar.dma_start(
             out=b1_raw[:].rearrange("p (g j) -> p g j", g=2),
             in_=bias1.rearrange("(g p j) -> p g j", g=2, p=P, j=4),
         )
-        w2_raw = consts.tile([P, 1024], BF16, name="w2_raw")
-        nc.scalar.dma_start(out=w2_raw[:], in_=weight2)
-        b2_raw = consts.tile([P, 1], BF16, name="b2_raw")
         nc.scalar.dma_start(out=b2_raw[:], in_=bias2.rearrange("(p o) -> p o", o=1))
+        load_w1(0)
+        nc.sync.dma_start(out=x_loads[0][0][:, 0:1024], in_=x_loads[0][1][:, 0:1024])
+        nc.sync.dma_start(out=x_loads[0][0][:, 1024:2048], in_=x_loads[0][1][:, 1024:2048])
+        load_w1(1)
+        nc.sync.dma_start(out=x_loads[1][0][:], in_=x_loads[1][1])
+        load_w1(2)
+        load_w1(3)
+        nc.sync.dma_start(out=w2_raw[:], in_=weight2)
+        nc.sync.dma_start(out=x_loads[2][0][:], in_=x_loads[2][1])
+        for chunk, src in x_loads[3:]:
+            nc.sync.dma_start(out=chunk[:], in_=src)
 
         ident = consts.tile([P, P], F32, name="ident")
         make_identity(nc, ident[:])
@@ -77,47 +88,56 @@ def tile_memoryefficientpatchdownscale_t_kernel(tc, x, weight1, bias1, weight2, 
         def bank(tag, bufs):
             return psum.tile([P, TOK], F32, tag=tag, bufs=bufs, name=tag)
 
-        def flip(views, dst_words, copy):
+        def flip(views, dst_words):
             pt = bank("o1", 5)
             for s, view in enumerate(views):
                 nc.tensor.transpose(out=pt[:, s * P : (s + 1) * P], in_=view, identity=ident[:])
-            copy(
+            nc.scalar.copy(
                 out=dst_words.rearrange("p (a h u) -> p a h u", a=2, u=2),
                 in_=pt[:].rearrange("p (a u h) -> p a h u", a=2, u=2),
             )
 
-        def flip_w1(g, a, copy):
+        def flip_w1(q):
+            g, a = divmod(q, 2)
             words = w1_raw[g][:].bitcast(F32).rearrange("p (j q u) -> p j u q", j=4, q=P, u=2)
             views = [words[:, 2 * a + jl, u, :] for jl in range(2) for u in range(2)]
-            first = (4 * g + 2 * a) * 256
-            flip(views, w1_grp[:].bitcast(F32)[:, first : first + 512], copy)
+            flip(views, w1_grp[:].bitcast(F32)[:, q * 512 : (q + 1) * 512])
 
-        def quant_w1(g):
+        def quant_w1(q):
             nc.vector.quantize_mx(
-                out=w1_codes[:, g * 512 : (g + 1) * 512].bitcast(FP8X4),
-                scales=w1_scales[:, g * 512 : (g + 1) * 512],
-                in_=w1_grp[:, g * 2048 : (g + 1) * 2048],
+                out=w1_codes[:, q * 256 : (q + 1) * 256].bitcast(FP8X4),
+                scales=w1_scales[:, q * 256 : (q + 1) * 256],
+                in_=w1_grp[:, q * 1024 : (q + 1) * 1024],
             )
 
         x_codes = {}
         x_grp = {}
 
-        def xr(n):
+        def xr(n, lo=0, hi=8):
             chunk, place = x_loc[n]
-            grp = work.tile([P, 2048], BF16, tag="x_grp", bufs=3, name="x_grp", align_bytes=64)
-            x_grp[n] = grp
+            if lo == 0:
+                x_grp[n] = work.tile([P, 2048], BF16, tag="x_grp", bufs=3, name="x_grp", align_bytes=64)
             nc.vector.tensor_copy(
-                out=grp[:].bitcast(F32).rearrange("p (i j u) -> p i j u", i=8, j=64, u=2),
+                out=x_grp[n][:]
+                .bitcast(F32)[:, lo * 128 : hi * 128]
+                .rearrange("p (i j u) -> p i j u", j=64, u=2),
                 in_=chunk[:]
-                .bitcast(F32)[:, place * 1024 : (place + 1) * 1024]
-                .rearrange("p (i u j) -> p i j u", i=8, u=2, j=64),
+                .bitcast(F32)[:, place * 1024 + lo * 128 : place * 1024 + hi * 128]
+                .rearrange("p (i u j) -> p i j u", u=2, j=64),
             )
 
-        def xq(n):
-            codes = work.tile([P, TOK], U32, tag="x_codes", bufs=4, name="x_codes", align_bytes=64)
-            scales = work.tile([P, TOK], U8, tag="x_scales", bufs=4, name="x_scales", align_bytes=64)
-            x_codes[n] = (codes, scales)
-            nc.vector.quantize_mx(out=codes[:].bitcast(FP8X4), scales=scales[:], in_=x_grp[n][:])
+        def xq(n, lo=0, hi=8):
+            if lo == 0:
+                x_codes[n] = (
+                    work.tile([P, TOK], U32, tag="x_codes", bufs=AHEAD + 2, name="x_codes", align_bytes=64),
+                    work.tile([P, TOK], U8, tag="x_scales", bufs=AHEAD + 2, name="x_scales", align_bytes=64),
+                )
+            codes, scales = x_codes[n]
+            nc.vector.quantize_mx(
+                out=codes[:, lo * 64 : hi * 64].bitcast(FP8X4),
+                scales=scales[:, lo * 64 : hi * 64],
+                in_=x_grp[n][:, lo * 256 : hi * 256],
+            )
 
         o1 = {}
         o2_raw = {}
@@ -141,27 +161,34 @@ def tile_memoryefficientpatchdownscale_t_kernel(tc, x, weight1, bias1, weight2, 
                 stop=True,
             )
 
-        def silu(n, t):
+        def silu(n, t, lo=0, hi=TOK):
             g, j = divmod(t, 4)
-            if j == 0:
+            if j == 0 and lo == 0:
                 o2_raw[(n, g)] = work.tile([P, 4, TOK], BF16, tag="o2_raw", bufs=4, name="o2_raw")
             nc.scalar.activation(
-                out=o2_raw[(n, g)][:, j, :], in_=o1[(n, t)][:], func=ACT.Silu, bias=b1[:, t : t + 1], scale=1.0
+                out=o2_raw[(n, g)][:, j, lo:hi],
+                in_=o1[(n, t)][:, lo:hi],
+                func=ACT.Silu,
+                bias=b1[:, t : t + 1],
+                scale=1.0,
             )
 
-        def pool(n):
+        def x_terms(n):
             chunk, place = x_loc[n]
-            acc = bank("pp", 1)
-            pooled_ps[n] = acc
-            view = chunk[:, place * 2048 : (place + 1) * 2048].rearrange(
+            return chunk[:, place * 2048 : (place + 1) * 2048].rearrange(
                 "p (i u j v) -> p u v i j", i=8, u=2, j=64, v=2
             )
-            terms = 3 if n == NT - 1 else 4
+
+        def pool(n, lo=0, hi=8):
+            if lo == 0:
+                pooled_ps[n] = bank("pp", 1)
+            view = x_terms(n)
+            terms = 3 if n == 0 else 4
             for s in range(terms):
                 nc.tensor.matmul(
-                    out=acc[:].rearrange("p (i j) -> p i j", i=8),
+                    out=pooled_ps[n][:, lo * 64 : hi * 64].rearrange("p (i j) -> p i j", j=64),
                     lhsT=quarter[:],
-                    rhs=view[:, s // 2, s % 2],
+                    rhs=view[:, s // 2, s % 2, lo:hi, :],
                     start=(s == 0),
                     stop=(s == terms - 1),
                 )
@@ -169,104 +196,145 @@ def tile_memoryefficientpatchdownscale_t_kernel(tc, x, weight1, bias1, weight2, 
         def pev(n):
             res = work.tile([P, TOK], F32, tag="pooled", bufs=3, name="pooled")
             pooled[n] = res
-            nc.scalar.activation(out=res[:], in_=pooled_ps[n][:], func=ACT.Identity, bias=b2[:, 0:1], scale=1.0)
+            if n == 0:
+                nc.vector.scalar_tensor_tensor(
+                    out=res[:].rearrange("p (i j) -> p i j", i=8),
+                    in0=x_terms(n)[:, 1, 1],
+                    scalar=0.25,
+                    in1=pooled_ps[n][:].rearrange("p (i j) -> p i j", i=8),
+                    op0=ALU.mult,
+                    op1=ALU.add,
+                )
+            elif n in POOLED_BY_VECTOR:
+                nc.vector.tensor_scalar_add(out=res[:], in0=pooled_ps[n][:], scalar1=b2[:, 0:1])
+            else:
+                nc.scalar.activation(out=res[:], in_=pooled_ps[n][:], func=ACT.Identity, bias=b2[:, 0:1], scale=1.0)
 
-        def pev_last(n):
-            chunk, place = x_loc[n]
-            view = chunk[:, place * 2048 : (place + 1) * 2048].rearrange(
-                "p (i u j v) -> p u v i j", i=8, u=2, j=64, v=2
-            )
-            res = work.tile([P, TOK], F32, tag="pooled", bufs=3, name="pooled")
-            pooled[n] = res
-            nc.vector.scalar_tensor_tensor(
-                out=res[:].rearrange("p (i j) -> p i j", i=8),
-                in0=view[:, 1, 1],
-                scalar=0.25,
-                in1=pooled_ps[n][:].rearrange("p (i j) -> p i j", i=8),
-                op0=ALU.mult,
-                op1=ALU.add,
-            )
-
-        def oreg(n, g):
-            grp = work.tile([P, 2048], BF16, tag="o2_grp", bufs=3, name="o2_grp", align_bytes=64)
-            o2_grp[(n, g)] = grp
-            nc.vector.tensor_copy(
-                out=grp[:].rearrange("p (c i t) -> p c t i", i=4, t=4),
-                in_=o2_raw[(n, g)][:].rearrange("p t (c i) -> p c t i", i=4),
+        def oreg(n, g, lo=0, hi=TOK, copy=nc.vector.tensor_copy):
+            if lo == 0:
+                o2_grp[(n, g)] = work.tile([P, 2048], BF16, tag="o2_grp", bufs=3, name="o2_grp", align_bytes=64)
+            copy(
+                out=o2_grp[(n, g)][:, 4 * lo : 4 * hi].rearrange("p (c i t) -> p c t i", i=4, t=4),
+                in_=o2_raw[(n, g)][:, :, lo:hi].rearrange("p t (c i) -> p c t i", i=4),
             )
 
-        def oq(n, g):
-            codes = work.tile([P, TOK], U32, tag="o2_codes", bufs=4, name="o2_codes", align_bytes=64)
-            scales = work.tile([P, TOK], U8, tag="o2_scales", bufs=4, name="o2_scales", align_bytes=64)
-            o2_codes[(n, g)] = (codes, scales)
-            nc.vector.quantize_mx(out=codes[:].bitcast(FP8X4), scales=scales[:], in_=o2_grp[(n, g)][:])
+        def oq(n, g, lo=0, hi=TOK):
+            if lo == 0:
+                o2_codes[(n, g)] = (
+                    work.tile([P, TOK], U32, tag="o2_codes", bufs=4, name="o2_codes", align_bytes=64),
+                    work.tile([P, TOK], U8, tag="o2_scales", bufs=4, name="o2_scales", align_bytes=64),
+                )
+            codes, scales = o2_codes[(n, g)]
+            nc.vector.quantize_mx(
+                out=codes[:, lo:hi].bitcast(FP8X4), scales=scales[:, lo:hi], in_=o2_grp[(n, g)][:, 4 * lo : 4 * hi]
+            )
 
-        def mm2(n):
-            acc = bank("o3", 2)
-            o3[n] = acc
+        def mm2(n, lo=0, hi=TOK):
+            if lo == 0:
+                o3[n] = bank("o3", 2)
             for g in range(2):
                 codes, scales = o2_codes[(n, g)]
                 nc.tensor.matmul_mx(
-                    out=acc[:],
+                    out=o3[n][:, lo:hi],
                     lhsT=w2_codes[:, g * P : (g + 1) * P].bitcast(FP8X4),
                     lhsT_scale=w2_scales[:, g * P : (g + 1) * P],
-                    rhs=codes[:].bitcast(FP8X4),
-                    rhs_scale=scales[:],
+                    rhs=codes[:, lo:hi].bitcast(FP8X4),
+                    rhs_scale=scales[:, lo:hi],
                     start=(g == 0),
                     stop=(g == 1),
                 )
 
-        def finish(n):
-            res = work.tile([P, TOK], F32, tag="res", bufs=4, name="res")
-            if n == NT - 1:
+        def finish(n, lo=0, hi=TOK):
+            res = work.tile([P, hi - lo], F32, tag="res%d" % (hi - lo), bufs=4, name="res")
+            if n == 0:
                 nc.vector.scalar_tensor_tensor(
-                    out=res[:], in0=o3[n][:], scalar=b2[:, 0:1], in1=pooled[n][:], op0=ALU.add, op1=ALU.add
+                    out=res[:], in0=o3[n][:, lo:hi], scalar=b2[:, 0:1], in1=pooled[n][:, lo:hi], op0=ALU.add, op1=ALU.add
                 )
             else:
-                nc.vector.tensor_tensor(out=res[:], in0=o3[n][:], in1=pooled[n][:], op=ALU.add)
+                nc.vector.tensor_tensor(out=res[:], in0=o3[n][:, lo:hi], in1=pooled[n][:, lo:hi], op=ALU.add)
             b, r = divmod(n, 8)
-            nc.sync.dma_start(out=out[b, :, 8 * r : 8 * r + 8, :].rearrange("c i j -> c (i j)"), in_=res[:])
+            nc.sync.dma_start(
+                out=out[b, :, 8 * r + lo // 64 : 8 * r + hi // 64, :].rearrange("c i j -> c (i j)"), in_=res[:]
+            )
 
-        flip_w1(0, 0, nc.scalar.copy)
-        flip_w1(0, 1, nc.scalar.copy)
-        xr(0)
-        xq(0)
+        flip_w1(0)
+        pool(0, 0, 4)
+        pool(0, 4, 8)
+        flip_w1(1)
+        xr(0, 0, 4)
+        xq(0, 0, 4)
+        xr(0, 4, 8)
         quant_w1(0)
+        xq(0, 4, 8)
         nc.vector.tensor_copy(out=b1[:], in_=b1_raw[:])
-        flip_w1(1, 0, nc.vector.tensor_copy)
-        flip_w1(1, 1, nc.vector.tensor_copy)
-        xr(1)
-        quant_w1(1)
-        xq(1)
-        w2_words = w2_raw[:].bitcast(F32).rearrange("p (g q u) -> p g u q", g=2, q=P, u=2)
-        flip([w2_words[:, g, u, :] for g in range(2) for u in range(2)], w2_grp[:].bitcast(F32), nc.vector.tensor_copy)
         nc.vector.tensor_copy(out=b2[:], in_=b2_raw[:])
-        nc.vector.quantize_mx(out=w2_codes[:].bitcast(FP8X4), scales=w2_scales[:], in_=w2_grp[:])
+        pev(0)
+        for t in range(2):
+            mm1(0, t)
+            silu(0, t)
+        quant_w1(1)
+        flip_w1(2)
+        flip_w1(3)
+        xr(1)
+        xq(1)
+        quant_w1(2)
+        xr(2)
+        quant_w1(3)
+        xq(2)
+        for t in range(2, 4):
+            mm1(0, t)
+            silu(0, t)
 
-        for n in range(NT + 1):
-            if n < NT:
+        LAST = NT - 1
+        HALF = TOK // 2
+        for n in range(LAST):
+            if n > 0:
                 for t in range(4):
                     mm1(n, t)
                     silu(n, t)
-                oreg(n, 0)
-                if n + 2 < NT:
-                    xr(n + 2)
-                oq(n, 0)
-                if n + 2 < NT:
-                    xq(n + 2)
-                for t in range(4, 8):
-                    mm1(n, t)
-                    silu(n, t)
-                pool(n)
-                if n < NT - 1:
-                    pev(n)
+            oreg(n, 0)
+            if n + AHEAD < NT:
+                xr(n + AHEAD)
+            oq(n, 0)
+            if n + AHEAD < NT:
+                xq(n + AHEAD)
+            for t in range(4, 8):
+                mm1(n, t)
+                silu(n, t)
+                if n == 0 and t == 5:
+                    w2_words = w2_raw[:].bitcast(F32).rearrange("p (g q u) -> p g u q", g=2, q=P, u=2)
+                    flip([w2_words[:, g, u, :] for g in range(2) for u in range(2)], w2_grp[:].bitcast(F32))
             if n >= 1:
+                pool(n)
+                pev(n)
                 mm2(n - 1)
-            if n < NT:
-                oreg(n, 1)
-            if n == NT:
-                pev_last(n - 1)
+            oreg(n, 1)
             if n >= 1:
                 finish(n - 1)
-            if n < NT:
-                oq(n, 1)
+            else:
+                nc.vector.quantize_mx(out=w2_codes[:].bitcast(FP8X4), scales=w2_scales[:], in_=w2_grp[:])
+            oq(n, 1)
+
+        for t in range(4):
+            mm1(LAST, t)
+            silu(LAST, t)
+        oreg(LAST, 0)
+        for t in range(4, 8):
+            mm1(LAST, t)
+        mm2(LAST - 1)
+        pool(LAST)
+        finish(LAST - 1)
+        oq(LAST, 0)
+        for t in range(4, 8):
+            silu(LAST, t, 0, HALF)
+        oreg(LAST, 1, 0, HALF)
+        for t in range(4, 8):
+            silu(LAST, t, HALF, TOK)
+        oreg(LAST, 1, HALF, TOK, nc.scalar.copy)
+        pev(LAST)
+        oq(LAST, 1, 0, HALF)
+        mm2(LAST, 0, HALF)
+        oq(LAST, 1, HALF, TOK)
+        mm2(LAST, HALF, TOK)
+        finish(LAST, 0, HALF)
+        finish(LAST, HALF, TOK)

@@ -211,35 +211,29 @@ def tile_memoryefficientpatchdownscale_t_kernel(tc, x, weight1, bias1, weight2, 
                 nc.scalar.activation(out=res[:], in_=pooled_ps[n][:], func=ACT.Identity, bias=b2[:, 0:1], scale=1.0)
 
         def oreg(n, g, lo=0, hi=TOK, copy=nc.vector.tensor_copy):
-            if lo == 0:
-                o2_grp[(n, g)] = work.tile([P, 2048], BF16, tag="o2_grp", bufs=3, name="o2_grp", align_bytes=64)
+            o2_grp[(n, g, lo)] = work.tile([P, 4 * (hi - lo)], BF16, tag="o2_grp", bufs=3, name="o2_grp", align_bytes=64)
             copy(
-                out=o2_grp[(n, g)][:, 4 * lo : 4 * hi].rearrange("p (c i t) -> p c t i", i=4, t=4),
+                out=o2_grp[(n, g, lo)][:].rearrange("p (c i t) -> p c t i", i=4, t=4),
                 in_=o2_raw[(n, g)][:, :, lo:hi].rearrange("p t (c i) -> p c t i", i=4),
             )
 
         def oq(n, g, lo=0, hi=TOK):
-            if lo == 0:
-                o2_codes[(n, g)] = (
-                    work.tile([P, TOK], U32, tag="o2_codes", bufs=4, name="o2_codes", align_bytes=64),
-                    work.tile([P, TOK], U8, tag="o2_scales", bufs=4, name="o2_scales", align_bytes=64),
-                )
-            codes, scales = o2_codes[(n, g)]
-            nc.vector.quantize_mx(
-                out=codes[:, lo:hi].bitcast(FP8X4), scales=scales[:, lo:hi], in_=o2_grp[(n, g)][:, 4 * lo : 4 * hi]
-            )
+            codes = work.tile([P, hi - lo], U32, tag="o2_codes", bufs=4, name="o2_codes", align_bytes=64)
+            scales = work.tile([P, hi - lo], U8, tag="o2_scales", bufs=4, name="o2_scales", align_bytes=64)
+            o2_codes[(n, g, lo)] = (codes, scales)
+            nc.vector.quantize_mx(out=codes[:].bitcast(FP8X4), scales=scales[:], in_=o2_grp[(n, g, lo)][:])
 
         def mm2(n, lo=0, hi=TOK):
-            if lo == 0:
-                o3[n] = bank("o3", 2)
+            o3[(n, lo)] = bank("o3", 2)
             for g in range(2):
-                codes, scales = o2_codes[(n, g)]
+                first = lo if (n, g, lo) in o2_codes else 0
+                codes, scales = o2_codes[(n, g, first)]
                 nc.tensor.matmul_mx(
-                    out=o3[n][:, lo:hi],
+                    out=o3[(n, lo)][:, 0 : hi - lo],
                     lhsT=w2_codes[:, g * P : (g + 1) * P].bitcast(FP8X4),
                     lhsT_scale=w2_scales[:, g * P : (g + 1) * P],
-                    rhs=codes[:, lo:hi].bitcast(FP8X4),
-                    rhs_scale=scales[:, lo:hi],
+                    rhs=codes[:, lo - first : hi - first].bitcast(FP8X4),
+                    rhs_scale=scales[:, lo - first : hi - first],
                     start=(g == 0),
                     stop=(g == 1),
                 )
@@ -248,10 +242,10 @@ def tile_memoryefficientpatchdownscale_t_kernel(tc, x, weight1, bias1, weight2, 
             res = work.tile([P, hi - lo], F32, tag="res%d" % (hi - lo), bufs=4, name="res")
             if n == 0:
                 nc.vector.scalar_tensor_tensor(
-                    out=res[:], in0=o3[n][:, lo:hi], scalar=b2[:, 0:1], in1=pooled[n][:, lo:hi], op0=ALU.add, op1=ALU.add
+                    out=res[:], in0=o3[(n, lo)][:, 0 : hi - lo], scalar=b2[:, 0:1], in1=pooled[n][:, lo:hi], op0=ALU.add, op1=ALU.add
                 )
             else:
-                nc.vector.tensor_tensor(out=res[:], in0=o3[n][:, lo:hi], in1=pooled[n][:, lo:hi], op=ALU.add)
+                nc.vector.tensor_tensor(out=res[:], in0=o3[(n, lo)][:, 0 : hi - lo], in1=pooled[n][:, lo:hi], op=ALU.add)
             b, r = divmod(n, 8)
             nc.sync.dma_start(
                 out=out[b, :, 8 * r + lo // 64 : 8 * r + hi // 64, :].rearrange("c i j -> c (i j)"), in_=res[:]
@@ -292,11 +286,15 @@ def tile_memoryefficientpatchdownscale_t_kernel(tc, x, weight1, bias1, weight2, 
                 for t in range(4):
                     mm1(n, t)
                     silu(n, t)
+            more_x = n + AHEAD < NT
             oreg(n, 0)
-            if n + AHEAD < NT:
+            if more_x:
                 xr(n + AHEAD)
+            else:
+                mm2(n - 1)
+                finish(n - 1)
             oq(n, 0)
-            if n + AHEAD < NT:
+            if more_x:
                 xq(n + AHEAD)
             for t in range(4, 8):
                 mm1(n, t)
@@ -306,13 +304,17 @@ def tile_memoryefficientpatchdownscale_t_kernel(tc, x, weight1, bias1, weight2, 
                     flip([w2_words[:, g, u, :] for g in range(2) for u in range(2)], w2_grp[:].bitcast(F32))
             if n >= 1:
                 pool(n)
-                pev(n)
-                mm2(n - 1)
+                if n not in POOLED_BY_VECTOR:
+                    pev(n)
+                if more_x:
+                    mm2(n - 1)
             oreg(n, 1)
-            if n >= 1:
-                finish(n - 1)
-            else:
+            if n == 0:
                 nc.vector.quantize_mx(out=w2_codes[:].bitcast(FP8X4), scales=w2_scales[:], in_=w2_grp[:])
+            elif more_x:
+                finish(n - 1)
+            elif n in POOLED_BY_VECTOR:
+                pev(n)
             oq(n, 1)
 
         for t in range(4):
@@ -335,6 +337,6 @@ def tile_memoryefficientpatchdownscale_t_kernel(tc, x, weight1, bias1, weight2, 
         oq(LAST, 1, 0, HALF)
         mm2(LAST, 0, HALF)
         oq(LAST, 1, HALF, TOK)
-        mm2(LAST, HALF, TOK)
         finish(LAST, 0, HALF)
+        mm2(LAST, HALF, TOK)
         finish(LAST, HALF, TOK)

@@ -18,7 +18,8 @@ AHEAD = 3
 FLOPS = 2 * 8192 * 512 * 1024 + 2 * 8192 * 1024 * 128
 
 CHUNKS = ((1, 1, 1, 1, 2, 2), (2, 2, 2, 2))
-POOLED_BY_VECTOR = (14,)
+POOLED_BY_VECTOR = ()
+XR_BY_SCALAR = (8,)
 
 
 def tile_memoryefficientpatchdownscale_t_kernel(tc, x, weight1, bias1, weight2, bias2, out):
@@ -113,11 +114,11 @@ def tile_memoryefficientpatchdownscale_t_kernel(tc, x, weight1, bias1, weight2, 
         x_codes = {}
         x_grp = {}
 
-        def xr(n, lo=0, hi=8):
+        def xr(n, lo=0, hi=8, copy=nc.vector.tensor_copy):
             chunk, place = x_loc[n]
             if lo == 0:
                 x_grp[n] = work.tile([P, 2048], BF16, tag="x_grp", bufs=3, name="x_grp", align_bytes=64)
-            nc.vector.tensor_copy(
+            copy(
                 out=x_grp[n][:]
                 .bitcast(F32)[:, lo * 128 : hi * 128]
                 .rearrange("p (i j u) -> p i j u", j=64, u=2),
@@ -282,20 +283,22 @@ def tile_memoryefficientpatchdownscale_t_kernel(tc, x, weight1, bias1, weight2, 
         LAST = NT - 1
         HALF = TOK // 2
         for n in range(LAST):
+            if n + AHEAD in XR_BY_SCALAR:
+                xr(n + AHEAD, 0, 8, nc.scalar.copy)
             if n > 0:
                 for t in range(4):
                     mm1(n, t)
                     silu(n, t)
-            more_x = n + AHEAD < NT
             oreg(n, 0)
-            if more_x:
-                xr(n + AHEAD)
-            else:
-                mm2(n - 1)
-                finish(n - 1)
-            oq(n, 0)
-            if more_x:
+            if n + AHEAD in XR_BY_SCALAR:
                 xq(n + AHEAD)
+                oq(n, 0)
+            else:
+                if n + AHEAD < NT:
+                    xr(n + AHEAD)
+                oq(n, 0)
+                if n + AHEAD < NT:
+                    xq(n + AHEAD)
             for t in range(4, 8):
                 mm1(n, t)
                 silu(n, t)
@@ -304,17 +307,13 @@ def tile_memoryefficientpatchdownscale_t_kernel(tc, x, weight1, bias1, weight2, 
                     flip([w2_words[:, g, u, :] for g in range(2) for u in range(2)], w2_grp[:].bitcast(F32))
             if n >= 1:
                 pool(n)
-                if n not in POOLED_BY_VECTOR:
-                    pev(n)
-                if more_x:
-                    mm2(n - 1)
-            oreg(n, 1)
-            if n == 0:
-                nc.vector.quantize_mx(out=w2_codes[:].bitcast(FP8X4), scales=w2_scales[:], in_=w2_grp[:])
-            elif more_x:
-                finish(n - 1)
-            elif n in POOLED_BY_VECTOR:
                 pev(n)
+                mm2(n - 1)
+            oreg(n, 1)
+            if n >= 1:
+                finish(n - 1)
+            else:
+                nc.vector.quantize_mx(out=w2_codes[:].bitcast(FP8X4), scales=w2_scales[:], in_=w2_grp[:])
             oq(n, 1)
 
         for t in range(4):

@@ -19,7 +19,6 @@ FLOPS = 2 * 8192 * 512 * 1024 + 2 * 8192 * 1024 * 128
 
 CHUNKS = ((1, 1, 1, 1, 2, 2), (2, 2, 2, 2))
 POOLED_BY_VECTOR = ()
-XR_BY_SCALAR = (8,)
 
 
 def tile_memoryefficientpatchdownscale_t_kernel(tc, x, weight1, bias1, weight2, bias2, out):
@@ -114,11 +113,11 @@ def tile_memoryefficientpatchdownscale_t_kernel(tc, x, weight1, bias1, weight2, 
         x_codes = {}
         x_grp = {}
 
-        def xr(n, lo=0, hi=8, copy=nc.vector.tensor_copy):
+        def xr(n, lo=0, hi=8):
             chunk, place = x_loc[n]
             if lo == 0:
                 x_grp[n] = work.tile([P, 2048], BF16, tag="x_grp", bufs=3, name="x_grp", align_bytes=64)
-            copy(
+            nc.vector.tensor_copy(
                 out=x_grp[n][:]
                 .bitcast(F32)[:, lo * 128 : hi * 128]
                 .rearrange("p (i j u) -> p i j u", j=64, u=2),
@@ -283,22 +282,16 @@ def tile_memoryefficientpatchdownscale_t_kernel(tc, x, weight1, bias1, weight2, 
         LAST = NT - 1
         HALF = TOK // 2
         for n in range(LAST):
-            if n + AHEAD in XR_BY_SCALAR:
-                xr(n + AHEAD, 0, 8, nc.scalar.copy)
             if n > 0:
                 for t in range(4):
                     mm1(n, t)
                     silu(n, t)
             oreg(n, 0)
-            if n + AHEAD in XR_BY_SCALAR:
+            if n + AHEAD < NT:
+                xr(n + AHEAD)
+            oq(n, 0)
+            if n + AHEAD < NT:
                 xq(n + AHEAD)
-                oq(n, 0)
-            else:
-                if n + AHEAD < NT:
-                    xr(n + AHEAD)
-                oq(n, 0)
-                if n + AHEAD < NT:
-                    xq(n + AHEAD)
             for t in range(4, 8):
                 mm1(n, t)
                 silu(n, t)

@@ -213,8 +213,8 @@ def tile_memoryefficientpatchdownscale_t_kernel(tc, x, weight1, bias1, weight2, 
         def oreg(n, g, lo=0, hi=TOK, copy=nc.vector.tensor_copy):
             o2_grp[(n, g, lo)] = work.tile([P, 4 * (hi - lo)], BF16, tag="o2_grp", bufs=3, name="o2_grp", align_bytes=64)
             copy(
-                out=o2_grp[(n, g, lo)][:].rearrange("p (c i t) -> p c t i", i=4, t=4),
-                in_=o2_raw[(n, g)][:, :, lo:hi].rearrange("p t (c i) -> p c t i", i=4),
+                out=o2_grp[(n, g, lo)][:].rearrange("p (c i t) -> p c t i", i=8, t=4),
+                in_=o2_raw[(n, g)][:, :, lo:hi].rearrange("p t (c i) -> p c t i", i=8),
             )
 
         def oq(n, g, lo=0, hi=TOK):

@@ -14,7 +14,6 @@ ALU = mybir.AluOpType
 P = 128
 TOK = 512
 NT = 16
-AHEAD = 3
 FLOPS = 2 * 8192 * 512 * 1024 + 2 * 8192 * 1024 * 128
 
 CHUNKS = ((1, 1, 1, 1, 2, 2), (2, 2, 2, 2))
@@ -50,20 +49,20 @@ def tile_memoryefficientpatchdownscale_t_kernel(tc, x, weight1, bias1, weight2, 
             g, a = divmod(q, 2)
             nc.sync.dma_start(out=w1_raw[g][:, a * 1024 : (a + 1) * 1024], in_=w1_src[g][:, a * 1024 : (a + 1) * 1024])
 
-        nc.scalar.dma_start(
-            out=b1_raw[:].rearrange("p (g j) -> p g j", g=2),
-            in_=bias1.rearrange("(g p j) -> p g j", g=2, p=P, j=4),
-        )
-        nc.scalar.dma_start(out=b2_raw[:], in_=bias2.rearrange("(p o) -> p o", o=1))
         load_w1(0)
         nc.sync.dma_start(out=x_loads[0][0][:, 0:1024], in_=x_loads[0][1][:, 0:1024])
         nc.sync.dma_start(out=x_loads[0][0][:, 1024:2048], in_=x_loads[0][1][:, 1024:2048])
+        nc.sync.dma_start(
+            out=b1_raw[:].rearrange("p (g j) -> p g j", g=2),
+            in_=bias1.rearrange("(g p j) -> p g j", g=2, p=P, j=4),
+        )
         load_w1(1)
         nc.sync.dma_start(out=x_loads[1][0][:], in_=x_loads[1][1])
         load_w1(2)
         load_w1(3)
-        nc.sync.dma_start(out=w2_raw[:], in_=weight2)
         nc.sync.dma_start(out=x_loads[2][0][:], in_=x_loads[2][1])
+        nc.sync.dma_start(out=w2_raw[:], in_=weight2)
+        nc.sync.dma_start(out=b2_raw[:], in_=bias2.rearrange("(p o) -> p o", o=1))
         for chunk, src in x_loads[3:]:
             nc.sync.dma_start(out=chunk[:], in_=src)
 
@@ -82,8 +81,6 @@ def tile_memoryefficientpatchdownscale_t_kernel(tc, x, weight1, bias1, weight2, 
         w2_grp = consts.tile([P, 1024], BF16, name="w2_grp", align_bytes=64)
         w2_codes = consts.tile([P, 256], U32, name="w2_codes", align_bytes=64)
         w2_scales = consts.tile([P, 256], U8, name="w2_scales", align_bytes=64)
-        b1 = consts.tile([P, 8], F32, name="b1")
-        b2 = consts.tile([P, 1], F32, name="b2")
 
         def bank(tag, bufs):
             return psum.tile([P, TOK], F32, tag=tag, bufs=bufs, name=tag)
@@ -113,11 +110,11 @@ def tile_memoryefficientpatchdownscale_t_kernel(tc, x, weight1, bias1, weight2, 
         x_codes = {}
         x_grp = {}
 
-        def xr(n, lo=0, hi=8):
+        def xr(n, lo=0, hi=8, copy=nc.vector.tensor_copy):
             chunk, place = x_loc[n]
             if lo == 0:
                 x_grp[n] = work.tile([P, 2048], BF16, tag="x_grp", bufs=3, name="x_grp", align_bytes=64)
-            nc.vector.tensor_copy(
+            copy(
                 out=x_grp[n][:]
                 .bitcast(F32)[:, lo * 128 : hi * 128]
                 .rearrange("p (i j u) -> p i j u", j=64, u=2),
@@ -129,8 +126,8 @@ def tile_memoryefficientpatchdownscale_t_kernel(tc, x, weight1, bias1, weight2, 
         def xq(n, lo=0, hi=8):
             if lo == 0:
                 x_codes[n] = (
-                    work.tile([P, TOK], U32, tag="x_codes", bufs=AHEAD + 2, name="x_codes", align_bytes=64),
-                    work.tile([P, TOK], U8, tag="x_scales", bufs=AHEAD + 2, name="x_scales", align_bytes=64),
+                    work.tile([P, TOK], U32, tag="x_codes", bufs=8, name="x_codes", align_bytes=64),
+                    work.tile([P, TOK], U8, tag="x_scales", bufs=8, name="x_scales", align_bytes=64),
                 )
             codes, scales = x_codes[n]
             nc.vector.quantize_mx(
@@ -163,13 +160,13 @@ def tile_memoryefficientpatchdownscale_t_kernel(tc, x, weight1, bias1, weight2, 
 
         def silu(n, t, lo=0, hi=TOK):
             g, j = divmod(t, 4)
-            if j == 0 and lo == 0:
-                o2_raw[(n, g)] = work.tile([P, 4, TOK], BF16, tag="o2_raw", bufs=4, name="o2_raw")
+            if t == 0:
+                o2_raw[n] = work.tile([P, 4, 2 * TOK], BF16, tag="o2_raw", bufs=3, name="o2_raw")
             nc.scalar.activation(
-                out=o2_raw[(n, g)][:, j, lo:hi],
+                out=o2_raw[n][:, j, g * TOK + lo : g * TOK + hi],
                 in_=o1[(n, t)][:, lo:hi],
                 func=ACT.Silu,
-                bias=b1[:, t : t + 1],
+                bias=b1_raw[:, t : t + 1],
                 scale=1.0,
             )
 
@@ -206,46 +203,51 @@ def tile_memoryefficientpatchdownscale_t_kernel(tc, x, weight1, bias1, weight2, 
                     op1=ALU.add,
                 )
             elif n in POOLED_BY_VECTOR:
-                nc.vector.tensor_scalar_add(out=res[:], in0=pooled_ps[n][:], scalar1=b2[:, 0:1])
+                nc.vector.tensor_copy(out=res[:], in_=pooled_ps[n][:])
             else:
-                nc.scalar.activation(out=res[:], in_=pooled_ps[n][:], func=ACT.Identity, bias=b2[:, 0:1], scale=1.0)
+                nc.scalar.copy(out=res[:], in_=pooled_ps[n][:])
 
-        def oreg(n, g, lo=0, hi=TOK, copy=nc.vector.tensor_copy):
-            o2_grp[(n, g, lo)] = work.tile([P, 4 * (hi - lo)], BF16, tag="o2_grp", bufs=3, name="o2_grp", align_bytes=64)
+        def oreg(n, lo, hi, copy=nc.vector.tensor_copy):
+            o2_grp[(n, lo)] = work.tile(
+                [P, 4 * (hi - lo)], BF16, tag="o2_grp%d" % (hi - lo), bufs=2, name="o2_grp", align_bytes=64
+            )
             copy(
-                out=o2_grp[(n, g, lo)][:].rearrange("p (c i t) -> p c t i", i=8, t=4),
-                in_=o2_raw[(n, g)][:, :, lo:hi].rearrange("p t (c i) -> p c t i", i=8),
+                out=o2_grp[(n, lo)][:].rearrange("p (c i t) -> p c t i", i=8, t=4),
+                in_=o2_raw[n][:, :, lo:hi].rearrange("p t (c i) -> p c t i", i=8),
             )
 
-        def oq(n, g, lo=0, hi=TOK):
-            codes = work.tile([P, hi - lo], U32, tag="o2_codes", bufs=4, name="o2_codes", align_bytes=64)
-            scales = work.tile([P, hi - lo], U8, tag="o2_scales", bufs=4, name="o2_scales", align_bytes=64)
-            o2_codes[(n, g, lo)] = (codes, scales)
-            nc.vector.quantize_mx(out=codes[:].bitcast(FP8X4), scales=scales[:], in_=o2_grp[(n, g, lo)][:])
+        def oq(n, lo, hi):
+            codes = work.tile([P, hi - lo], U32, tag="o2_codes%d" % (hi - lo), bufs=4, name="o2_codes", align_bytes=64)
+            scales = work.tile([P, hi - lo], U8, tag="o2_scales%d" % (hi - lo), bufs=4, name="o2_scales", align_bytes=64)
+            o2_codes.setdefault(n, []).append((lo, hi, codes, scales))
+            nc.vector.quantize_mx(out=codes[:].bitcast(FP8X4), scales=scales[:], in_=o2_grp[(n, lo)][:])
 
         def mm2(n, lo=0, hi=TOK):
             o3[(n, lo)] = bank("o3", 2)
             for g in range(2):
-                first = lo if (n, g, lo) in o2_codes else 0
-                codes, scales = o2_codes[(n, g, first)]
-                nc.tensor.matmul_mx(
-                    out=o3[(n, lo)][:, 0 : hi - lo],
-                    lhsT=w2_codes[:, g * P : (g + 1) * P].bitcast(FP8X4),
-                    lhsT_scale=w2_scales[:, g * P : (g + 1) * P],
-                    rhs=codes[:, lo - first : hi - first].bitcast(FP8X4),
-                    rhs_scale=scales[:, lo - first : hi - first],
-                    start=(g == 0),
-                    stop=(g == 1),
-                )
+                for first, end, codes, scales in o2_codes[n]:
+                    if first <= g * TOK + lo and g * TOK + hi <= end:
+                        start = g * TOK + lo - first
+                        nc.tensor.matmul_mx(
+                            out=o3[(n, lo)][:, 0 : hi - lo],
+                            lhsT=w2_codes[:, g * P : (g + 1) * P].bitcast(FP8X4),
+                            lhsT_scale=w2_scales[:, g * P : (g + 1) * P],
+                            rhs=codes[:, start : start + hi - lo].bitcast(FP8X4),
+                            rhs_scale=scales[:, start : start + hi - lo],
+                            start=(g == 0),
+                            stop=(g == 1),
+                        )
 
         def finish(n, lo=0, hi=TOK):
             res = work.tile([P, hi - lo], F32, tag="res%d" % (hi - lo), bufs=4, name="res")
-            if n == 0:
-                nc.vector.scalar_tensor_tensor(
-                    out=res[:], in0=o3[(n, lo)][:, 0 : hi - lo], scalar=b2[:, 0:1], in1=pooled[n][:, lo:hi], op0=ALU.add, op1=ALU.add
-                )
-            else:
-                nc.vector.tensor_tensor(out=res[:], in0=o3[(n, lo)][:, 0 : hi - lo], in1=pooled[n][:, lo:hi], op=ALU.add)
+            nc.vector.scalar_tensor_tensor(
+                out=res[:],
+                in0=o3[(n, lo)][:, 0 : hi - lo],
+                scalar=b2_raw[:, 0:1],
+                in1=pooled[n][:, lo:hi],
+                op0=ALU.add,
+                op1=ALU.add,
+            )
             b, r = divmod(n, 8)
             nc.sync.dma_start(
                 out=out[b, :, 8 * r + lo // 64 : 8 * r + hi // 64, :].rearrange("c i j -> c (i j)"), in_=res[:]
@@ -254,81 +256,95 @@ def tile_memoryefficientpatchdownscale_t_kernel(tc, x, weight1, bias1, weight2, 
         flip_w1(0)
         pool(0, 0, 4)
         pool(0, 4, 8)
-        flip_w1(1)
         xr(0, 0, 4)
+        xr(0, 4, 8, nc.scalar.copy)
+        flip_w1(1)
         xq(0, 0, 4)
-        xr(0, 4, 8)
         quant_w1(0)
         xq(0, 4, 8)
-        nc.vector.tensor_copy(out=b1[:], in_=b1_raw[:])
-        nc.vector.tensor_copy(out=b2[:], in_=b2_raw[:])
         pev(0)
         for t in range(2):
             mm1(0, t)
             silu(0, t)
+        xr(1)
         quant_w1(1)
         flip_w1(2)
         flip_w1(3)
-        xr(1)
         xq(1)
-        quant_w1(2)
         xr(2)
+        quant_w1(2)
         quant_w1(3)
         xq(2)
         for t in range(2, 4):
             mm1(0, t)
             silu(0, t)
 
+        oreg(0, 0, TOK)
+        xr(3)
+        oq(0, 0, TOK)
+        xq(3)
+        for t in range(4, 8):
+            mm1(0, t)
+            silu(0, t)
+            if t == 5:
+                w2_words = w2_raw[:].bitcast(F32).rearrange("p (g q u) -> p g u q", g=2, q=P, u=2)
+                flip([w2_words[:, g, u, :] for g in range(2) for u in range(2)], w2_grp[:].bitcast(F32))
+        oreg(0, TOK, 2 * TOK)
+        nc.vector.quantize_mx(out=w2_codes[:].bitcast(FP8X4), scales=w2_scales[:], in_=w2_grp[:])
+        oq(0, TOK, 2 * TOK)
+
         LAST = NT - 1
         HALF = TOK // 2
-        for n in range(LAST):
-            if n > 0:
-                for t in range(4):
-                    mm1(n, t)
-                    silu(n, t)
-            oreg(n, 0)
-            if n + AHEAD < NT:
-                xr(n + AHEAD)
-            oq(n, 0)
-            if n + AHEAD < NT:
-                xq(n + AHEAD)
-            for t in range(4, 8):
+        for n in range(1, LAST):
+            for t in range(8):
                 mm1(n, t)
                 silu(n, t)
-                if n == 0 and t == 5:
-                    w2_words = w2_raw[:].bitcast(F32).rearrange("p (g q u) -> p g u q", g=2, q=P, u=2)
-                    flip([w2_words[:, g, u, :] for g in range(2) for u in range(2)], w2_grp[:].bitcast(F32))
-            if n >= 1:
-                pool(n)
-                pev(n)
-                mm2(n - 1)
-            oreg(n, 1)
-            if n >= 1:
-                finish(n - 1)
+                if t == 3 and n >= 2:
+                    mm2(n - 2)
+            pool(n)
+            pev(n)
+            if n == 1:
+                xr(4)
+                xr(5)
+                xq(4)
+                xq(5)
             else:
-                nc.vector.quantize_mx(out=w2_codes[:].bitcast(FP8X4), scales=w2_scales[:], in_=w2_grp[:])
-            oq(n, 1)
+                oreg(n - 1, 0, 2 * TOK)
+                if n + 4 < NT:
+                    xr(n + 4)
+                    oq(n - 1, 0, 2 * TOK)
+                    finish(n - 2)
+                    xq(n + 4)
+                else:
+                    finish(n - 2)
+                    oq(n - 1, 0, 2 * TOK)
+        oreg(LAST - 1, 0, TOK)
+        oq(LAST - 1, 0, TOK)
 
         for t in range(4):
             mm1(LAST, t)
             silu(LAST, t)
-        oreg(LAST, 0)
+        mm2(LAST - 2)
+        oreg(LAST - 1, TOK, 2 * TOK)
+        finish(LAST - 2)
+        oq(LAST - 1, TOK, 2 * TOK)
+        oreg(LAST, 0, TOK)
         for t in range(4, 8):
             mm1(LAST, t)
         mm2(LAST - 1)
         pool(LAST)
         finish(LAST - 1)
-        oq(LAST, 0)
+        oq(LAST, 0, TOK)
         for t in range(4, 8):
             silu(LAST, t, 0, HALF)
-        oreg(LAST, 1, 0, HALF)
+        oreg(LAST, TOK, TOK + HALF)
         for t in range(4, 8):
             silu(LAST, t, HALF, TOK)
-        oreg(LAST, 1, HALF, TOK, nc.scalar.copy)
+        oreg(LAST, TOK + HALF, 2 * TOK, nc.scalar.copy)
         pev(LAST)
-        oq(LAST, 1, 0, HALF)
+        oq(LAST, TOK, TOK + HALF)
         mm2(LAST, 0, HALF)
-        oq(LAST, 1, HALF, TOK)
+        oq(LAST, TOK + HALF, 2 * TOK)
         finish(LAST, 0, HALF)
         mm2(LAST, HALF, TOK)
         finish(LAST, HALF, TOK)

@@ -59,8 +59,8 @@ def tile_memoryefficientpatchdownscale_t_kernel(tc, x, weight1, bias1, weight2, 
         load_w1(1)
         nc.sync.dma_start(out=x_loads[1][0][:], in_=x_loads[1][1])
         load_w1(2)
-        load_w1(3)
         nc.sync.dma_start(out=x_loads[2][0][:], in_=x_loads[2][1])
+        load_w1(3)
         nc.sync.dma_start(out=w2_raw[:], in_=weight2)
         nc.sync.dma_start(out=b2_raw[:], in_=bias2.rearrange("(p o) -> p o", o=1))
         for chunk, src in x_loads[3:]:
@@ -110,11 +110,11 @@ def tile_memoryefficientpatchdownscale_t_kernel(tc, x, weight1, bias1, weight2, 
         x_codes = {}
         x_grp = {}
 
-        def xr(n, lo=0, hi=8, copy=nc.vector.tensor_copy):
+        def xr(n, lo=0, hi=8):
             chunk, place = x_loc[n]
             if lo == 0:
                 x_grp[n] = work.tile([P, 2048], BF16, tag="x_grp", bufs=3, name="x_grp", align_bytes=64)
-            copy(
+            nc.vector.tensor_copy(
                 out=x_grp[n][:]
                 .bitcast(F32)[:, lo * 128 : hi * 128]
                 .rearrange("p (i j u) -> p i j u", j=64, u=2),
@@ -223,7 +223,7 @@ def tile_memoryefficientpatchdownscale_t_kernel(tc, x, weight1, bias1, weight2, 
             nc.vector.quantize_mx(out=codes[:].bitcast(FP8X4), scales=scales[:], in_=o2_grp[(n, lo)][:])
 
         def mm2(n, lo=0, hi=TOK):
-            o3[(n, lo)] = bank("o3", 2)
+            o3[(n, lo)] = bank("o1", 5) if hi == 384 else bank("o3", 2)
             for g in range(2):
                 for first, end, codes, scales in o2_codes[n]:
                     if first <= g * TOK + lo and g * TOK + hi <= end:
@@ -256,10 +256,10 @@ def tile_memoryefficientpatchdownscale_t_kernel(tc, x, weight1, bias1, weight2, 
         flip_w1(0)
         pool(0, 0, 4)
         pool(0, 4, 8)
-        xr(0, 0, 4)
-        xr(0, 4, 8, nc.scalar.copy)
         flip_w1(1)
+        xr(0, 0, 4)
         xq(0, 0, 4)
+        xr(0, 4, 8)
         quant_w1(0)
         xq(0, 4, 8)
         pev(0)
@@ -269,15 +269,16 @@ def tile_memoryefficientpatchdownscale_t_kernel(tc, x, weight1, bias1, weight2, 
         xr(1)
         quant_w1(1)
         flip_w1(2)
-        flip_w1(3)
         xq(1)
+        mm1(0, 2)
+        silu(0, 2)
+        mm1(0, 3)
+        flip_w1(3)
+        silu(0, 3)
         xr(2)
         quant_w1(2)
-        quant_w1(3)
         xq(2)
-        for t in range(2, 4):
-            mm1(0, t)
-            silu(0, t)
+        quant_w1(3)
 
         oreg(0, 0, TOK)
         xr(3)
@@ -294,7 +295,6 @@ def tile_memoryefficientpatchdownscale_t_kernel(tc, x, weight1, bias1, weight2, 
         oq(0, TOK, 2 * TOK)
 
         LAST = NT - 1
-        HALF = TOK // 2
         for n in range(1, LAST):
             for t in range(8):
                 mm1(n, t)
@@ -334,17 +334,17 @@ def tile_memoryefficientpatchdownscale_t_kernel(tc, x, weight1, bias1, weight2, 
         mm2(LAST - 1)
         pool(LAST)
         finish(LAST - 1)
+        for t in range(4, 8):
+            silu(LAST, t, 0, 256)
+        oreg(LAST, 512, 768)
         oq(LAST, 0, TOK)
-        for t in range(4, 8):
-            silu(LAST, t, 0, HALF)
-        oreg(LAST, TOK, TOK + HALF)
-        for t in range(4, 8):
-            silu(LAST, t, HALF, TOK)
-        oreg(LAST, TOK + HALF, 2 * TOK, nc.scalar.copy)
+        for lo, hi in ((256, 384), (384, 512)):
+            for t in range(4, 8):
+                silu(LAST, t, lo, hi)
+            oreg(LAST, TOK + lo, TOK + hi, nc.scalar.copy)
         pev(LAST)
-        oq(LAST, TOK, TOK + HALF)
-        mm2(LAST, 0, HALF)
-        oq(LAST, TOK + HALF, 2 * TOK)
-        finish(LAST, 0, HALF)
-        mm2(LAST, HALF, TOK)
-        finish(LAST, HALF, TOK)
+        for lo, hi in ((0, 256), (256, 384), (384, 512)):
+            oq(LAST, TOK + lo, TOK + hi)
+            mm2(LAST, lo, hi)
+        for lo, hi in ((0, 256), (256, 384), (384, 512)):
+            finish(LAST, lo, hi)

@@ -113,7 +113,8 @@ def tile_memoryefficientpatchdownscale_t_kernel(tc, x, weight1, bias1, weight2, 
         def xr(n, lo=0, hi=8):
             chunk, place = x_loc[n]
             if lo == 0:
-                x_grp[n] = work.tile([P, 2048], BF16, tag="x_grp", bufs=3, name="x_grp", align_bytes=64)
+                width = 2048 * max(1, hi // 8)
+                x_grp[n] = work.tile([P, width], BF16, tag="x_grp%d" % width, bufs=4096 // width, name="x_grp", align_bytes=64)
             nc.vector.tensor_copy(
                 out=x_grp[n][:]
                 .bitcast(F32)[:, lo * 128 : hi * 128]
@@ -125,11 +126,14 @@ def tile_memoryefficientpatchdownscale_t_kernel(tc, x, weight1, bias1, weight2, 
 
         def xq(n, lo=0, hi=8):
             if lo == 0:
-                x_codes[n] = (
-                    work.tile([P, TOK], U32, tag="x_codes", bufs=8, name="x_codes", align_bytes=64),
-                    work.tile([P, TOK], U8, tag="x_scales", bufs=8, name="x_scales", align_bytes=64),
-                )
-            codes, scales = x_codes[n]
+                tiles = max(1, hi // 8)
+                width = TOK * tiles
+                bufs = 4 if tiles == 1 else 3
+                codes = work.tile([P, width], U32, tag="x_codes%d" % width, bufs=bufs, name="x_codes", align_bytes=64)
+                scales = work.tile([P, width], U8, tag="x_scales%d" % width, bufs=bufs, name="x_scales", align_bytes=64)
+                for place in range(tiles):
+                    x_codes[n + place] = (codes, scales, place * TOK)
+            codes, scales, start = x_codes[n]
             nc.vector.quantize_mx(
                 out=codes[:, lo * 64 : hi * 64].bitcast(FP8X4),
                 scales=scales[:, lo * 64 : hi * 64],
@@ -147,13 +151,13 @@ def tile_memoryefficientpatchdownscale_t_kernel(tc, x, weight1, bias1, weight2, 
         def mm1(n, t):
             acc = bank("o1", 5)
             o1[(n, t)] = acc
-            codes, scales = x_codes[n]
+            codes, scales, start = x_codes[n]
             nc.tensor.matmul_mx(
                 out=acc[:],
                 lhsT=w1_codes[:, t * P : (t + 1) * P].bitcast(FP8X4),
                 lhsT_scale=w1_scales[:, t * P : (t + 1) * P],
-                rhs=codes[:].bitcast(FP8X4),
-                rhs_scale=scales[:],
+                rhs=codes[:, start : start + TOK].bitcast(FP8X4),
+                rhs_scale=scales[:, start : start + TOK],
                 start=True,
                 stop=True,
             )
@@ -217,13 +221,13 @@ def tile_memoryefficientpatchdownscale_t_kernel(tc, x, weight1, bias1, weight2, 
             )
 
         def oq(n, lo, hi):
-            codes = work.tile([P, hi - lo], U32, tag="o2_codes%d" % (hi - lo), bufs=4, name="o2_codes", align_bytes=64)
-            scales = work.tile([P, hi - lo], U8, tag="o2_scales%d" % (hi - lo), bufs=4, name="o2_scales", align_bytes=64)
+            codes = work.tile([P, hi - lo], U32, tag="o2_codes%d" % (hi - lo), bufs=2 if hi - lo > TOK else 4, name="o2_codes", align_bytes=64)
+            scales = work.tile([P, hi - lo], U8, tag="o2_scales%d" % (hi - lo), bufs=2 if hi - lo > TOK else 4, name="o2_scales", align_bytes=64)
             o2_codes.setdefault(n, []).append((lo, hi, codes, scales))
             nc.vector.quantize_mx(out=codes[:].bitcast(FP8X4), scales=scales[:], in_=o2_grp[(n, lo)][:])
 
         def mm2(n, lo=0, hi=TOK):
-            o3[(n, lo)] = bank("o1", 5) if hi == 384 else bank("o3", 2)
+            o3[(n, lo)] = bank("o3", 2)
             for g in range(2):
                 for first, end, codes, scales in o2_codes[n]:
                     if first <= g * TOK + lo and g * TOK + hi <= end:
@@ -292,29 +296,27 @@ def tile_memoryefficientpatchdownscale_t_kernel(tc, x, weight1, bias1, weight2, 
                 flip([w2_words[:, g, u, :] for g in range(2) for u in range(2)], w2_grp[:].bitcast(F32))
         oreg(0, TOK, 2 * TOK)
         nc.vector.quantize_mx(out=w2_codes[:].bitcast(FP8X4), scales=w2_scales[:], in_=w2_grp[:])
+        xr(4, 0, 16)
         oq(0, TOK, 2 * TOK)
+        xq(4, 0, 16)
 
         LAST = NT - 1
+        HALF = TOK // 2
         for n in range(1, LAST):
             for t in range(8):
                 mm1(n, t)
                 silu(n, t)
-                if t == 3 and n >= 2:
+                if t == 5 and n >= 2:
                     mm2(n - 2)
             pool(n)
             pev(n)
-            if n == 1:
-                xr(4)
-                xr(5)
-                xq(4)
-                xq(5)
-            else:
+            if n >= 2:
                 oreg(n - 1, 0, 2 * TOK)
-                if n + 4 < NT:
-                    xr(n + 4)
+                if n % 2 == 0 and n + 4 < NT:
+                    xr(n + 4, 0, 16)
                     oq(n - 1, 0, 2 * TOK)
                     finish(n - 2)
-                    xq(n + 4)
+                    xq(n + 4, 0, 16)
                 else:
                     finish(n - 2)
                     oq(n - 1, 0, 2 * TOK)
@@ -335,16 +337,15 @@ def tile_memoryefficientpatchdownscale_t_kernel(tc, x, weight1, bias1, weight2, 
         pool(LAST)
         finish(LAST - 1)
         for t in range(4, 8):
-            silu(LAST, t, 0, 256)
-        oreg(LAST, 512, 768)
+            silu(LAST, t, 0, HALF)
+        oreg(LAST, TOK, TOK + HALF)
         oq(LAST, 0, TOK)
-        for lo, hi in ((256, 384), (384, 512)):
-            for t in range(4, 8):
-                silu(LAST, t, lo, hi)
-            oreg(LAST, TOK + lo, TOK + hi, nc.scalar.copy)
+        for t in range(4, 8):
+            silu(LAST, t, HALF, TOK)
+        oreg(LAST, TOK + HALF, 2 * TOK, nc.scalar.copy)
         pev(LAST)
-        for lo, hi in ((0, 256), (256, 384), (384, 512)):
-            oq(LAST, TOK + lo, TOK + hi)
-            mm2(LAST, lo, hi)
-        for lo, hi in ((0, 256), (256, 384), (384, 512)):
-            finish(LAST, lo, hi)
+        for lo in (0, HALF):
+            oq(LAST, TOK + lo, TOK + lo + HALF)
+            mm2(LAST, lo, lo + HALF)
+        for lo in (0, HALF):
+            finish(LAST, lo, lo + HALF)

@@ -59,8 +59,8 @@ def tile_memoryefficientpatchdownscale_t_kernel(tc, x, weight1, bias1, weight2, 
         load_w1(1)
         nc.sync.dma_start(out=x_loads[1][0][:], in_=x_loads[1][1])
         load_w1(2)
-        nc.sync.dma_start(out=x_loads[2][0][:], in_=x_loads[2][1])
         load_w1(3)
+        nc.sync.dma_start(out=x_loads[2][0][:], in_=x_loads[2][1])
         nc.sync.dma_start(out=w2_raw[:], in_=weight2)
         nc.sync.dma_start(out=b2_raw[:], in_=bias2.rearrange("(p o) -> p o", o=1))
         for chunk, src in x_loads[3:]:
@@ -110,12 +110,12 @@ def tile_memoryefficientpatchdownscale_t_kernel(tc, x, weight1, bias1, weight2, 
         x_codes = {}
         x_grp = {}
 
-        def xr(n, lo=0, hi=8):
+        def xr(n, lo=0, hi=8, copy=nc.vector.tensor_copy):
             chunk, place = x_loc[n]
             if lo == 0:
                 width = 2048 * max(1, hi // 8)
                 x_grp[n] = work.tile([P, width], BF16, tag="x_grp%d" % width, bufs=4096 // width, name="x_grp", align_bytes=64)
-            nc.vector.tensor_copy(
+            copy(
                 out=x_grp[n][:]
                 .bitcast(F32)[:, lo * 128 : hi * 128]
                 .rearrange("p (i j u) -> p i j u", j=64, u=2),
@@ -260,10 +260,10 @@ def tile_memoryefficientpatchdownscale_t_kernel(tc, x, weight1, bias1, weight2, 
         flip_w1(0)
         pool(0, 0, 4)
         pool(0, 4, 8)
-        flip_w1(1)
         xr(0, 0, 4)
+        xr(0, 4, 8, nc.scalar.copy)
+        flip_w1(1)
         xq(0, 0, 4)
-        xr(0, 4, 8)
         quant_w1(0)
         xq(0, 4, 8)
         pev(0)
@@ -273,16 +273,15 @@ def tile_memoryefficientpatchdownscale_t_kernel(tc, x, weight1, bias1, weight2, 
         xr(1)
         quant_w1(1)
         flip_w1(2)
-        xq(1)
-        mm1(0, 2)
-        silu(0, 2)
-        mm1(0, 3)
         flip_w1(3)
-        silu(0, 3)
+        xq(1)
         xr(2)
         quant_w1(2)
-        xq(2)
         quant_w1(3)
+        xq(2)
+        for t in range(2, 4):
+            mm1(0, t)
+            silu(0, t)
 
         oreg(0, 0, TOK)
         xr(3)
@@ -321,13 +320,13 @@ def tile_memoryefficientpatchdownscale_t_kernel(tc, x, weight1, bias1, weight2, 
                     finish(n - 2)
                     oq(n - 1, 0, 2 * TOK)
         oreg(LAST - 1, 0, TOK)
-        oq(LAST - 1, 0, TOK)
 
         for t in range(4):
             mm1(LAST, t)
             silu(LAST, t)
         mm2(LAST - 2)
         oreg(LAST - 1, TOK, 2 * TOK)
+        oq(LAST - 1, 0, TOK)
         finish(LAST - 2)
         oq(LAST - 1, TOK, 2 * TOK)
         oreg(LAST, 0, TOK)

from contextlib import ExitStack

import concourse.mybir as mybir
from concourse.masks import make_identity

F32 = mybir.dt.float32
BF16 = mybir.dt.bfloat16
U32 = mybir.dt.uint32
U8 = mybir.dt.uint8
FP8X4 = mybir.dt.float8_e4m3fn_x4
ACT = mybir.ActivationFunctionType
ALU = mybir.AluOpType

P = 128
TOK = 512
NT = 16
FLOPS = 2 * 8192 * 512 * 1024 + 2 * 8192 * 1024 * 128

CHUNKS = ((1, 1, 1, 1, 2, 2), (2, 2, 2, 2))
POOLED_BY_VECTOR = ()


def tile_memoryefficientpatchdownscale_t_kernel(tc, x, weight1, bias1, weight2, bias2, out):
    nc = tc.nc
    with ExitStack() as ctx:
        consts = ctx.enter_context(tc.tile_pool(name="consts", bufs=1))
        work = ctx.enter_context(tc.tile_pool(name="work", bufs=3))
        psum = ctx.enter_context(tc.psum_pool(name="psum", bufs=1))
        ctx.enter_context(tc.manual_schedule())

        w1_src = weight1.rearrange("(g p j) k -> g p (j k)", g=2, p=P, j=4)
        w1_raw = [consts.tile([P, 2048], BF16, name="w1_raw%d" % g) for g in range(2)]
        w2_raw = consts.tile([P, 1024], BF16, name="w2_raw")
        b1_raw = consts.tile([P, 8], BF16, name="b1_raw")
        b2_raw = consts.tile([P, 1], BF16, name="b2_raw")
        x_loc = []
        x_loads = []
        for b in range(2):
            first = 0
            for count in CHUNKS[b]:
                chunk = consts.tile([P, count * 2048], BF16, name="x_%d_%d" % (b, first))
                src = x[b, :, 16 * first : 16 * (first + count), :].rearrange("c h w -> c (h w)")
                x_loads.append((chunk, src))
                for place in range(count):
                    x_loc.append((chunk, place))
                first += count

        def load_w1(q):
            g, a = divmod(q, 2)
            nc.sync.dma_start(out=w1_raw[g][:, a * 1024 : (a + 1) * 1024], in_=w1_src[g][:, a * 1024 : (a + 1) * 1024])

        load_w1(0)
        nc.sync.dma_start(out=x_loads[0][0][:, 0:1024], in_=x_loads[0][1][:, 0:1024])
        nc.sync.dma_start(out=x_loads[0][0][:, 1024:2048], in_=x_loads[0][1][:, 1024:2048])
        nc.sync.dma_start(
            out=b1_raw[:].rearrange("p (g j) -> p g j", g=2),
            in_=bias1.rearrange("(g p j) -> p g j", g=2, p=P, j=4),
        )
        load_w1(1)
        nc.sync.dma_start(out=x_loads[1][0][:], in_=x_loads[1][1])
        load_w1(2)
        load_w1(3)
        nc.sync.dma_start(out=x_loads[2][0][:], in_=x_loads[2][1])
        nc.sync.dma_start(out=w2_raw[:], in_=weight2)
        nc.sync.dma_start(out=b2_raw[:], in_=bias2.rearrange("(p o) -> p o", o=1))
        for chunk, src in x_loads[3:]:
            nc.sync.dma_start(out=chunk[:], in_=src)

        ident = consts.tile([P, P], F32, name="ident")
        make_identity(nc, ident[:])
        warm = consts.tile([P, 1], F32, name="warm")
        nc.vector.memset(warm[:], 0.0)
        warm_out = consts.tile([P, 1], F32, name="warm_out")
        nc.scalar.activation(out=warm_out[:], in_=warm[:], func=ACT.Silu)
        quarter = consts.tile([P, P], BF16, name="quarter")
        nc.vector.tensor_scalar_mul(out=quarter[:], in0=ident[:], scalar1=0.25)

        w1_grp = consts.tile([P, 4096], BF16, name="w1_grp", align_bytes=64)
        w1_codes = consts.tile([P, 1024], U32, name="w1_codes", align_bytes=64)
        w1_scales = consts.tile([P, 1024], U8, name="w1_scales", align_bytes=64)
        w2_grp = consts.tile([P, 1024], BF16, name="w2_grp", align_bytes=64)
        w2_codes = consts.tile([P, 256], U32, name="w2_codes", align_bytes=64)
        w2_scales = consts.tile([P, 256], U8, name="w2_scales", align_bytes=64)

        def bank(tag, bufs):
            return psum.tile([P, TOK], F32, tag=tag, bufs=bufs, name=tag)

        def flip(views, dst_words):
            pt = bank("o1", 5)
            for s, view in enumerate(views):
                nc.tensor.transpose(out=pt[:, s * P : (s + 1) * P], in_=view, identity=ident[:])
            nc.scalar.copy(
                out=dst_words.rearrange("p (a h u) -> p a h u", a=2, u=2),
                in_=pt[:].rearrange("p (a u h) -> p a h u", a=2, u=2),
            )

        def flip_w1(q):
            g, a = divmod(q, 2)
            words = w1_raw[g][:].bitcast(F32).rearrange("p (j q u) -> p j u q", j=4, q=P, u=2)
            views = [words[:, 2 * a + jl, u, :] for jl in range(2) for u in range(2)]
            flip(views, w1_grp[:].bitcast(F32)[:, q * 512 : (q + 1) * 512])

        def quant_w1(q):
            nc.vector.quantize_mx(
                out=w1_codes[:, q * 256 : (q + 1) * 256].bitcast(FP8X4),
                scales=w1_scales[:, q * 256 : (q + 1) * 256],
                in_=w1_grp[:, q * 1024 : (q + 1) * 1024],
            )

        x_codes = {}
        x_grp = {}

        def xr(n, lo=0, hi=8, copy=nc.vector.tensor_copy):
            chunk, place = x_loc[n]
            if lo == 0:
                width = 2048 * max(1, hi // 8)
                x_grp[n] = work.tile([P, width], BF16, tag="x_grp%d" % width, bufs=4096 // width, name="x_grp", align_bytes=64)
            copy(
                out=x_grp[n][:]
                .bitcast(F32)[:, lo * 128 : hi * 128]
                .rearrange("p (i j u) -> p i j u", j=64, u=2),
                in_=chunk[:]
                .bitcast(F32)[:, place * 1024 + lo * 128 : place * 1024 + hi * 128]
                .rearrange("p (i u j) -> p i j u", u=2, j=64),
            )

        def xq(n, lo=0, hi=8):
            if lo == 0:
                tiles = max(1, hi // 8)
                width = TOK * tiles
                bufs = 4 if tiles == 1 else 3
                codes = work.tile([P, width], U32, tag="x_codes%d" % width, bufs=bufs, name="x_codes", align_bytes=64)
                scales = work.tile([P, width], U8, tag="x_scales%d" % width, bufs=bufs, name="x_scales", align_bytes=64)
                for place in range(tiles):
                    x_codes[n + place] = (codes, scales, place * TOK)
            codes, scales, start = x_codes[n]
            nc.vector.quantize_mx(
                out=codes[:, lo * 64 : hi * 64].bitcast(FP8X4),
                scales=scales[:, lo * 64 : hi * 64],
                in_=x_grp[n][:, lo * 256 : hi * 256],
            )

        o1 = {}
        o2_raw = {}
        o2_grp = {}
        o2_codes = {}
        pooled_ps = {}
        pooled = {}
        o3 = {}

        def mm1(n, t):
            acc = bank("o1", 5)
            o1[(n, t)] = acc
            codes, scales, start = x_codes[n]
            nc.tensor.matmul_mx(
                out=acc[:],
                lhsT=w1_codes[:, t * P : (t + 1) * P].bitcast(FP8X4),
                lhsT_scale=w1_scales[:, t * P : (t + 1) * P],
                rhs=codes[:, start : start + TOK].bitcast(FP8X4),
                rhs_scale=scales[:, start : start + TOK],
                start=True,
                stop=True,
            )

        def silu(n, t, lo=0, hi=TOK):
            g, j = divmod(t, 4)
            if t == 0:
                o2_raw[n] = work.tile([P, 4, 2 * TOK], BF16, tag="o2_raw", bufs=3, name="o2_raw")
            nc.scalar.activation(
                out=o2_raw[n][:, j, g * TOK + lo : g * TOK + hi],
                in_=o1[(n, t)][:, lo:hi],
                func=ACT.Silu,
                bias=b1_raw[:, t : t + 1],
                scale=1.0,
            )

        def x_terms(n):
            chunk, place = x_loc[n]
            return chunk[:, place * 2048 : (place + 1) * 2048].rearrange(
                "p (i u j v) -> p u v i j", i=8, u=2, j=64, v=2
            )

        def pool(n, lo=0, hi=8):
            if lo == 0:
                pooled_ps[n] = bank("pp", 1)
            view = x_terms(n)
            terms = 3 if n == 0 else 4
            for s in range(terms):
                nc.tensor.matmul(
                    out=pooled_ps[n][:, lo * 64 : hi * 64].rearrange("p (i j) -> p i j", j=64),
                    lhsT=quarter[:],
                    rhs=view[:, s // 2, s % 2, lo:hi, :],
                    start=(s == 0),
                    stop=(s == terms - 1),
                )

        def pev(n):
            res = work.tile([P, TOK], F32, tag="pooled", bufs=3, name="pooled")
            pooled[n] = res
            if n == 0:
                nc.vector.scalar_tensor_tensor(
                    out=res[:].rearrange("p (i j) -> p i j", i=8),
                    in0=x_terms(n)[:, 1, 1],
                    scalar=0.25,
                    in1=pooled_ps[n][:].rearrange("p (i j) -> p i j", i=8),
                    op0=ALU.mult,
                    op1=ALU.add,
                )
            elif n in POOLED_BY_VECTOR:
                nc.vector.tensor_copy(out=res[:], in_=pooled_ps[n][:])
            else:
                nc.scalar.copy(out=res[:], in_=pooled_ps[n][:])

        def oreg(n, lo, hi, copy=nc.vector.tensor_copy):
            o2_grp[(n, lo)] = work.tile(
                [P, 4 * (hi - lo)], BF16, tag="o2_grp%d" % (hi - lo), bufs=2, name="o2_grp", align_bytes=64
            )
            copy(
                out=o2_grp[(n, lo)][:].rearrange("p (c i t) -> p c t i", i=8, t=4),
                in_=o2_raw[n][:, :, lo:hi].rearrange("p t (c i) -> p c t i", i=8),
            )

        def oq(n, lo, hi):
            codes = work.tile([P, hi - lo], U32, tag="o2_codes%d" % (hi - lo), bufs=2 if hi - lo > TOK else 4, name="o2_codes", align_bytes=64)
            scales = work.tile([P, hi - lo], U8, tag="o2_scales%d" % (hi - lo), bufs=2 if hi - lo > TOK else 4, name="o2_scales", align_bytes=64)
            o2_codes.setdefault(n, []).append((lo, hi, codes, scales))
            nc.vector.quantize_mx(out=codes[:].bitcast(FP8X4), scales=scales[:], in_=o2_grp[(n, lo)][:])

        def mm2(n, lo=0, hi=TOK):
            o3[(n, lo)] = bank("o3", 2)
            for g in range(2):
                for first, end, codes, scales in o2_codes[n]:
                    if first <= g * TOK + lo and g * TOK + hi <= end:
                        start = g * TOK + lo - first
                        nc.tensor.matmul_mx(
                            out=o3[(n, lo)][:, 0 : hi - lo],
                            lhsT=w2_codes[:, g * P : (g + 1) * P].bitcast(FP8X4),
                            lhsT_scale=w2_scales[:, g * P : (g + 1) * P],
                            rhs=codes[:, start : start + hi - lo].bitcast(FP8X4),
                            rhs_scale=scales[:, start : start + hi - lo],
                            start=(g == 0),
                            stop=(g == 1),
                        )

        def finish(n, lo=0, hi=TOK):
            res = work.tile([P, hi - lo], F32, tag="res%d" % (hi - lo), bufs=4, name="res")
            nc.vector.scalar_tensor_tensor(
                out=res[:],
                in0=o3[(n, lo)][:, 0 : hi - lo],
                scalar=b2_raw[:, 0:1],
                in1=pooled[n][:, lo:hi],
                op0=ALU.add,
                op1=ALU.add,
            )
            b, r = divmod(n, 8)
            nc.sync.dma_start(
                out=out[b, :, 8 * r + lo // 64 : 8 * r + hi // 64, :].rearrange("c i j -> c (i j)"), in_=res[:]
            )

        flip_w1(0)
        pool(0, 0, 4)
        pool(0, 4, 8)
        xr(0, 0, 4)
        xr(0, 4, 8, nc.scalar.copy)
        flip_w1(1)
        xq(0, 0, 4)
        quant_w1(0)
        xq(0, 4, 8)
        pev(0)
        for t in range(2):
            mm1(0, t)
            silu(0, t)
        xr(1)
        quant_w1(1)
        flip_w1(2)
        flip_w1(3)
        xq(1)
        xr(2)
        quant_w1(2)
        quant_w1(3)
        xq(2)
        for t in range(2, 4):
            mm1(0, t)
            silu(0, t)

        oreg(0, 0, TOK)
        xr(3)
        oq(0, 0, TOK)
        xq(3)
        for t in range(4, 8):
            mm1(0, t)
            silu(0, t)
            if t == 5:
                w2_words = w2_raw[:].bitcast(F32).rearrange("p (g q u) -> p g u q", g=2, q=P, u=2)
                flip([w2_words[:, g, u, :] for g in range(2) for u in range(2)], w2_grp[:].bitcast(F32))
        oreg(0, TOK, 2 * TOK)
        nc.vector.quantize_mx(out=w2_codes[:].bitcast(FP8X4), scales=w2_scales[:], in_=w2_grp[:])
        xr(4, 0, 16)
        oq(0, TOK, 2 * TOK)
        xq(4, 0, 16)

        LAST = NT - 1
        HALF = TOK // 2
        for n in range(1, LAST):
            for t in range(8):
                mm1(n, t)
                silu(n, t)
                if t == 5 and n >= 2:
                    mm2(n - 2)
            pool(n)
            pev(n)
            if n >= 2:
                oreg(n - 1, 0, 2 * TOK)
                if n % 2 == 0 and n + 4 < NT:
                    xr(n + 4, 0, 16)
                    oq(n - 1, 0, 2 * TOK)
                    finish(n - 2)
                    xq(n + 4, 0, 16)
                else:
                    finish(n - 2)
                    oq(n - 1, 0, 2 * TOK)
        oreg(LAST - 1, 0, TOK)

        for t in range(4):
            mm1(LAST, t)
            silu(LAST, t)
        mm2(LAST - 2)
        oreg(LAST - 1, TOK, 2 * TOK)
        oq(LAST - 1, 0, TOK)
        finish(LAST - 2)
        oq(LAST - 1, TOK, 2 * TOK)
        oreg(LAST, 0, TOK)
        for t in range(4, 8):
            mm1(LAST, t)
        mm2(LAST - 1)
        pool(LAST)
        finish(LAST - 1)
        for t in range(4, 8):
            silu(LAST, t, 0, HALF)
        oreg(LAST, TOK, TOK + HALF)
        oq(LAST, 0, TOK)
        for t in range(4, 8):
            silu(LAST, t, HALF, TOK)
        oreg(LAST, TOK + HALF, 2 * TOK, nc.scalar.copy)
        pev(LAST)
        for lo in (0, HALF):
            oq(LAST, TOK + lo, TOK + lo + HALF)
            mm2(LAST, lo, lo + HALF)
        for lo in (0, HALF):
            finish(LAST, lo, lo + HALF)
